import numpy as np
import ml_dtypes


def mxq(x, axis, fmt="e4m3"):
    dtype, down = {"e4m3": (ml_dtypes.float8_e4m3fn, 7), "e5m2": (ml_dtypes.float8_e5m2, 14)}[fmt]
    v = np.moveaxis(np.asarray(x, np.float32).astype(ml_dtypes.bfloat16).astype(np.float64), axis, -1)
    blocks = v.reshape(v.shape[:-1] + (-1, 32))
    amax = np.abs(blocks).max(-1, keepdims=True)
    byte = np.maximum(np.where(amax > 0, np.frexp(amax)[1] - 1 + 127, 0) - down, 1)
    scale = np.exp2(byte - 127.0)
    codes = (blocks / scale).astype(np.float32).astype(dtype).astype(np.float64)
    return np.moveaxis((codes * scale).reshape(v.shape), -1, axis)


WIDE = False


def mx_kscale(k):
    if not WIDE:
        return np.ones(k)
    levels = np.array([10, -10, 5, -5, 0])
    a = np.random.permutation(np.resize(levels, k // 512 * 4)).reshape(k // 512, 4)
    idx = np.arange(k)
    return np.exp2(a[idx // 512, idx % 128 // 32])


BF16 = ml_dtypes.bfloat16


def bf(x):
    return np.asarray(x, np.float32).astype(BF16)


def f64(x):
    return np.asarray(x).astype(np.float64)


E2M1 = np.array([0.0, 0.5, 1.0, 1.5, 2.0, 3.0, 4.0, 6.0, -0.0, -0.5, -1.0, -1.5, -2.0, -3.0, -4.0, -6.0])


def pack_weight(w, fmt):
    k, n = w.shape
    w = f64(bf(w)).reshape(k // 32, 32, n)
    amax = np.abs(w).max(1)
    if fmt == "e4m3":
        byte = np.frexp(amax)[1] - 1 + 127 - 7
    else:
        mant, ex = np.frexp(amax / 6.0)
        byte = np.where(mant > 0.5, ex, ex - 1) + 127
    byte = np.clip(np.where(amax > 0, byte, 1), 1, 254)
    scaled = (w * np.exp2(127.0 - byte)[:, None, :]).reshape(k, n).astype(np.float32)
    by_word = np.ascontiguousarray(scaled.reshape(k // 512, 128, 4, n).transpose(0, 1, 3, 2))
    if fmt == "e4m3":
        words = by_word.astype(ml_dtypes.float8_e4m3fn).view(np.uint8)
    else:
        c = by_word.astype(ml_dtypes.float4_e2m1fn).view(np.uint8) & 0xF
        words = c[..., 0::2] | (c[..., 1::2] << 4)
    return np.ascontiguousarray(words), np.ascontiguousarray(byte.astype(np.uint8).reshape(k // 512, 16, n))


def unpack_weight(words, scales, fmt):
    g, p, n, _ = words.shape
    if fmt == "e4m3":
        vals = np.ascontiguousarray(words).view(ml_dtypes.float8_e4m3fn).astype(np.float64)
    else:
        nib = np.empty((g, p, n, 4), np.uint8)
        nib[..., 0::2] = words & 0xF
        nib[..., 1::2] = words >> 4
        vals = E2M1[nib]
    vals = vals * np.repeat(np.exp2(scales.astype(np.float64) - 127.0), 8, axis=1)[..., None]
    return vals.transpose(0, 1, 3, 2).reshape(g * 512, n)


N, D, T, H, DH = 1, 1024, 512, 2, 512
EPS = 1e-12
A = 6.0
R = 0.2
FMT = "e4m3"


def l2norm(x):
    n = np.sqrt(np.sum(x * x, axis=-1, keepdims=True))
    return x / np.maximum(n, EPS)


def setup_inputs():
    s = mx_kscale(D)
    rgb = bf(np.random.standard_normal((N, D, T)) * R * s[None, :, None])
    proj = np.random.standard_normal((H, D, DH)) / (R * np.sqrt(D)) / s[None, :, None]
    atte = np.random.standard_normal((H, DH, DH)) * A
    proj_words, proj_scales = pack_weight(proj.reshape(-1, DH), FMT)
    atte_words, atte_scales = pack_weight(atte.reshape(-1, DH), FMT)
    return {"rgb": rgb,
            "rgb_proj_words": proj_words, "rgb_proj_scales": proj_scales,
            "atte_w_words": atte_words, "atte_w_scales": atte_scales}


def reference(rgb, rgb_proj_words, rgb_proj_scales, atte_w_words, atte_w_scales):
    rgb_t = f64(rgb).swapaxes(1, 2)
    proj = unpack_weight(rgb_proj_words, rgb_proj_scales, FMT).reshape(H, D, DH)
    atte = unpack_weight(atte_w_words, atte_w_scales, FMT).reshape(H, DH, DH)
    p = mxq(rgb_t, 2, "e4m3")[:, None] @ proj[None]
    o_rgb = l2norm(p)
    q_bil = mxq(o_rgb, 3, "e4m3") @ atte[None]
    return o_rgb, q_bil

@@ -1,0 +1,164 @@
+from contextlib import ExitStack
+
+import concourse.mybir as mybir
+from concourse.masks import make_identity
+
+F32 = mybir.dt.float32
+BF16 = mybir.dt.bfloat16
+I32 = mybir.dt.int32
+U8 = mybir.dt.uint8
+FP8X4 = mybir.dt.float8_e4m3fn_x4
+ACT = mybir.ActivationFunctionType
+ALU = mybir.AluOpType
+
+P = 128
+PACK = 4
+K_PASS = P * PACK
+D, T, H, DH = 1024, 512, 2, 512
+D_PASSES = D // K_PASS
+T_TILES = T // P
+UNITS = H * T_TILES
+EPS = 1e-12
+QUADRANTS = 4
+VECTOR_COLUMNS = 384
+
+FLOPS = 2 * H * T * D * DH + 2 * H * T * DH * DH
+
+
+def tile_mca_pa_e_kernel(
+    tc, rgb, rgb_proj_words, rgb_proj_scales, atte_w_words, atte_w_scales, out_0, out_1
+):
+    nc = tc.nc
+    with ExitStack() as stack:
+        keep = stack.enter_context(tc.tile_pool(name="keep", bufs=1))
+        per_unit = stack.enter_context(tc.tile_pool(name="per_unit", bufs=UNITS))
+        p_banks = stack.enter_context(tc.psum_pool(name="p_banks", bufs=4))
+        t_banks = stack.enter_context(tc.psum_pool(name="t_banks", bufs=2))
+        q_banks = stack.enter_context(tc.psum_pool(name="q_banks", bufs=2))
+
+        proj_planes = keep.tile([P, DH], U8, align_bytes=64)
+        atte_planes = keep.tile([P, DH], U8, align_bytes=64)
+        nc.vector.memset(proj_planes[:].bitcast(I32), 0)
+        nc.vector.memset(atte_planes[:].bitcast(I32), 0)
+        one = keep.tile([P, 1], F32)
+        warm = keep.tile([P, 1], F32)
+        nc.vector.memset(one[:], 1.0)
+        nc.scalar.activation(out=warm[:], in_=one[:], func=ACT.Sqrt)
+        identity = keep.tile([P, P], F32)
+        make_identity(nc, identity[:])
+
+        rgb_raw = keep.tile([P, D_PASSES, PACK, T], BF16)
+        rgb_rows = rgb.rearrange("o (g p j) w -> (o g) p j w", g=D_PASSES, p=P, j=PACK)
+        for g in range(D_PASSES):
+            nc.sync.dma_start(out=rgb_raw[:, g], in_=rgb_rows[g])
+        for quadrant in range(QUADRANTS):
+            nc.sync.dma_start(
+                out=proj_planes[32 * quadrant : 32 * quadrant + 16, :].bitcast(I32),
+                in_=rgb_proj_scales[:, 4 * quadrant : 4 * quadrant + 4, :].bitcast(I32),
+            )
+        proj_words = keep.tile([P, H * D_PASSES, DH], I32, align_bytes=64)
+        proj_bytes = rgb_proj_words.rearrange("g p n t -> p g (n t)").bitcast(I32)
+        for h in range(H):
+            passes = slice(h * D_PASSES, (h + 1) * D_PASSES)
+            nc.sync.dma_start(out=proj_words[:, passes, :], in_=proj_bytes[:, passes, :])
+        for quadrant in range(QUADRANTS):
+            nc.sync.dma_start(
+                out=atte_planes[32 * quadrant : 32 * quadrant + 8, :].bitcast(I32),
+                in_=atte_w_scales[:, 4 * quadrant : 4 * quadrant + 4, :].bitcast(I32),
+            )
+        atte_words = keep.tile([P, H, DH], I32, align_bytes=64)
+        nc.sync.dma_start(
+            out=atte_words[:], in_=atte_w_words.rearrange("g p n t -> p g (n t)").bitcast(I32)
+        )
+
+        rgb_grouped = keep.tile([P, D_PASSES, T, PACK], BF16, align_bytes=64)
+        rgb_codes = keep.tile([P, D_PASSES, T], I32, align_bytes=64)
+        rgb_scales = keep.tile([P, D_PASSES, T], U8, align_bytes=64)
+        for g in range(D_PASSES):
+            nc.vector.tensor_copy(
+                out=rgb_grouped[:, g, :VECTOR_COLUMNS, :],
+                in_=rgb_raw[:, g, :, :VECTOR_COLUMNS].rearrange("p j w -> p w j"),
+            )
+            nc.scalar.copy(
+                out=rgb_grouped[:, g, VECTOR_COLUMNS:, :],
+                in_=rgb_raw[:, g, :, VECTOR_COLUMNS:].rearrange("p j w -> p w j"),
+            )
+        for g in range(D_PASSES):
+            nc.vector.quantize_mx(
+                out=rgb_codes[:, g, :].bitcast(FP8X4),
+                scales=rgb_scales[:, g, :],
+                in_=rgb_grouped[:, g].rearrange("p w j -> p (w j)"),
+            )
+
+        for unit in range(UNITS):
+            h, t_tile = divmod(unit, T_TILES)
+            steps = slice(t_tile * P, (t_tile + 1) * P)
+
+            p_bank = p_banks.tile([P, DH], F32)
+            for g in range(D_PASSES):
+                weight_pass = h * D_PASSES + g
+                nc.tensor.matmul_mx(
+                    out=p_bank[:],
+                    lhsT=rgb_codes[:, g, steps].bitcast(FP8X4),
+                    lhsT_scale=rgb_scales[:, g, steps],
+                    rhs=proj_words[:, weight_pass, :].bitcast(FP8X4),
+                    rhs_scale=proj_planes[4 * weight_pass : P, :],
+                    start=(g == 0),
+                    stop=(g == D_PASSES - 1),
+                )
+
+            squares = per_unit.tile([P, DH], BF16)
+            sum_squares = per_unit.tile([P, 1], F32)
+            nc.scalar.activation(
+                out=squares[:], in_=p_bank[:], func=ACT.Square, accum_out=sum_squares[:]
+            )
+            floored = per_unit.tile([P, 1], F32)
+            nc.vector.tensor_scalar_max(out=floored[:], in0=sum_squares[:], scalar1=EPS * EPS)
+            inverse = per_unit.tile([P, 1], F32)
+            nc.vector.reciprocal(out=inverse[:], in_=floored[:])
+            inverse_norm = per_unit.tile([P, 1], F32)
+            nc.scalar.activation(out=inverse_norm[:], in_=inverse[:], func=ACT.Sqrt)
+
+            o_f32 = per_unit.tile([P, DH], F32)
+            nc.vector.tensor_scalar_mul(out=o_f32[:], in0=p_bank[:], scalar1=inverse_norm[:])
+            nc.sync.dma_start(out=out_0[0, h, steps, :], in_=o_f32[:])
+
+            o_bf16 = per_unit.tile([P, 2, P, 2], BF16)
+            nc.gpsimd.tensor_scalar(
+                out=o_bf16[:],
+                in0=o_f32[:].rearrange("p (q s e) -> p s q e", s=2, e=2),
+                scalar1=1.0,
+                scalar2=0.0,
+                op0=ALU.mult,
+                op1=ALU.add,
+            )
+
+            pairs_t = t_banks.tile([P, 2, P], F32)
+            for s in range(2):
+                nc.tensor.transpose(
+                    out=pairs_t[:, s, :],
+                    in_=o_bf16[:, s].rearrange("p q e -> p (q e)").bitcast(F32),
+                    identity=identity[:],
+                )
+            o_grouped = per_unit.tile([P, P * PACK], BF16, align_bytes=64)
+            nc.vector.tensor_copy(
+                out=o_grouped[:].bitcast(F32).rearrange("q (t s) -> q t s", s=2),
+                in_=pairs_t[:].rearrange("q s t -> q t s"),
+            )
+            o_codes = per_unit.tile([P, P], I32, align_bytes=64)
+            o_scales = per_unit.tile([P, P], U8, align_bytes=64)
+            nc.vector.quantize_mx(out=o_codes[:].bitcast(FP8X4), scales=o_scales[:], in_=o_grouped[:])
+
+            q_bank = q_banks.tile([P, DH], F32)
+            nc.tensor.matmul_mx(
+                out=q_bank[:],
+                lhsT=o_codes[:].bitcast(FP8X4),
+                lhsT_scale=o_scales[:],
+                rhs=atte_words[:, h, :].bitcast(FP8X4),
+                rhs_scale=atte_planes[4 * h : P, :],
+                start=True,
+                stop=True,
+            )
+            q_f32 = per_unit.tile([P, DH], F32)
+            nc.scalar.copy(out=q_f32[:], in_=q_bank[:])
+            nc.sync.dma_start(out=out_1[0, h, steps, :], in_=q_f32[:])

@@ -20,7 +20,7 @@ T_TILES = T // P
 UNITS = H * T_TILES
 EPS = 1e-12
 QUADRANTS = 4
-VECTOR_COLUMNS = 384
+HALF_T = T // 2
 
 FLOPS = 2 * H * T * D * DH + 2 * H * T * DH * DH
 
@@ -31,10 +31,10 @@ def tile_mca_pa_e_kernel(
     nc = tc.nc
     with ExitStack() as stack:
         keep = stack.enter_context(tc.tile_pool(name="keep", bufs=1))
-        per_unit = stack.enter_context(tc.tile_pool(name="per_unit", bufs=UNITS))
         p_banks = stack.enter_context(tc.psum_pool(name="p_banks", bufs=4))
         t_banks = stack.enter_context(tc.psum_pool(name="t_banks", bufs=2))
         q_banks = stack.enter_context(tc.psum_pool(name="q_banks", bufs=2))
+        stack.enter_context(tc.manual_schedule())
 
         proj_planes = keep.tile([P, DH], U8, align_bytes=64)
         atte_planes = keep.tile([P, DH], U8, align_bytes=64)
@@ -74,27 +74,49 @@ def tile_mca_pa_e_kernel(
         rgb_grouped = keep.tile([P, D_PASSES, T, PACK], BF16, align_bytes=64)
         rgb_codes = keep.tile([P, D_PASSES, T], I32, align_bytes=64)
         rgb_scales = keep.tile([P, D_PASSES, T], U8, align_bytes=64)
-        for g in range(D_PASSES):
-            nc.vector.tensor_copy(
-                out=rgb_grouped[:, g, :VECTOR_COLUMNS, :],
-                in_=rgb_raw[:, g, :, :VECTOR_COLUMNS].rearrange("p j w -> p w j"),
+
+        def regroup_rgb(copy, g, steps):
+            copy(
+                out=rgb_grouped[:, g, steps, :],
+                in_=rgb_raw[:, g, :, steps].rearrange("p j w -> p w j"),
             )
-            nc.scalar.copy(
-                out=rgb_grouped[:, g, VECTOR_COLUMNS:, :],
-                in_=rgb_raw[:, g, :, VECTOR_COLUMNS:].rearrange("p j w -> p w j"),
-            )
-        for g in range(D_PASSES):
+
+        def quantise_rgb(g, steps):
             nc.vector.quantize_mx(
-                out=rgb_codes[:, g, :].bitcast(FP8X4),
-                scales=rgb_scales[:, g, :],
-                in_=rgb_grouped[:, g].rearrange("p w j -> p (w j)"),
+                out=rgb_codes[:, g, steps].bitcast(FP8X4),
+                scales=rgb_scales[:, g, steps],
+                in_=rgb_grouped[:, g, steps, :].rearrange("p w j -> p (w j)"),
             )
 
-        for unit in range(UNITS):
-            h, t_tile = divmod(unit, T_TILES)
-            steps = slice(t_tile * P, (t_tile + 1) * P)
+        first_half, second_half = slice(0, HALF_T), slice(HALF_T, T)
+        for g in range(D_PASSES):
+            regroup_rgb(nc.vector.tensor_copy, g, first_half)
+            regroup_rgb(nc.scalar.copy, g, second_half)
+            quantise_rgb(g, first_half)
+        for g in range(D_PASSES):
+            quantise_rgb(g, second_half)
 
+        squares = keep.tile([P, UNITS, DH], BF16)
+        sum_squares = keep.tile([P, UNITS], F32)
+        floored = keep.tile([P, UNITS], F32)
+        inverse = keep.tile([P, UNITS], F32)
+        inverse_norm = keep.tile([P, UNITS], F32)
+        o_f32 = keep.tile([P, UNITS, DH], F32)
+        o_bf16 = keep.tile([P, UNITS, 2, P, 2], BF16)
+        o_grouped = keep.tile([P, UNITS, P * PACK], BF16, align_bytes=64)
+        o_codes = keep.tile([P, UNITS, P], I32, align_bytes=64)
+        o_scales = keep.tile([P, UNITS, P], U8, align_bytes=64)
+        q_f32 = keep.tile([P, UNITS, DH], F32)
+        p_bank_of, pairs_of, q_bank_of = {}, {}, {}
+
+        def head_and_steps(unit):
+            h, t_tile = divmod(unit, T_TILES)
+            return h, slice(t_tile * P, (t_tile + 1) * P)
+
+        def project(unit):
+            h, steps = head_and_steps(unit)
             p_bank = p_banks.tile([P, DH], F32)
+            p_bank_of[unit] = p_bank
             for g in range(D_PASSES):
                 weight_pass = h * D_PASSES + g
                 nc.tensor.matmul_mx(
@@ -107,58 +129,91 @@ def tile_mca_pa_e_kernel(
                     stop=(g == D_PASSES - 1),
                 )
 
-            squares = per_unit.tile([P, DH], BF16)
-            sum_squares = per_unit.tile([P, 1], F32)
+        def square(unit):
             nc.scalar.activation(
-                out=squares[:], in_=p_bank[:], func=ACT.Square, accum_out=sum_squares[:]
+                out=squares[:, unit, :],
+                in_=p_bank_of[unit][:],
+                func=ACT.Square,
+                accum_out=sum_squares[:, unit : unit + 1],
             )
-            floored = per_unit.tile([P, 1], F32)
-            nc.vector.tensor_scalar_max(out=floored[:], in0=sum_squares[:], scalar1=EPS * EPS)
-            inverse = per_unit.tile([P, 1], F32)
-            nc.vector.reciprocal(out=inverse[:], in_=floored[:])
-            inverse_norm = per_unit.tile([P, 1], F32)
-            nc.scalar.activation(out=inverse_norm[:], in_=inverse[:], func=ACT.Sqrt)
 
-            o_f32 = per_unit.tile([P, DH], F32)
-            nc.vector.tensor_scalar_mul(out=o_f32[:], in0=p_bank[:], scalar1=inverse_norm[:])
-            nc.sync.dma_start(out=out_0[0, h, steps, :], in_=o_f32[:])
+        def invert(unit):
+            column = slice(unit, unit + 1)
+            nc.vector.tensor_scalar_max(
+                out=floored[:, column], in0=sum_squares[:, column], scalar1=EPS * EPS
+            )
+            nc.vector.reciprocal(out=inverse[:, column], in_=floored[:, column])
 
-            o_bf16 = per_unit.tile([P, 2, P, 2], BF16)
+        def root(unit):
+            column = slice(unit, unit + 1)
+            nc.scalar.activation(out=inverse_norm[:, column], in_=inverse[:, column], func=ACT.Sqrt)
+
+        def normalise(unit):
+            h, steps = head_and_steps(unit)
+            nc.vector.tensor_scalar_mul(
+                out=o_f32[:, unit, :],
+                in0=p_bank_of[unit][:],
+                scalar1=inverse_norm[:, unit : unit + 1],
+            )
+            nc.sync.dma_start(out=out_0[0, h, steps, :], in_=o_f32[:, unit, :])
+
+        def round_to_bf16(unit):
             nc.gpsimd.tensor_scalar(
-                out=o_bf16[:],
-                in0=o_f32[:].rearrange("p (q s e) -> p s q e", s=2, e=2),
+                out=o_bf16[:, unit],
+                in0=o_f32[:, unit, :].rearrange("p (q s e) -> p s q e", s=2, e=2),
                 scalar1=1.0,
                 scalar2=0.0,
                 op0=ALU.mult,
                 op1=ALU.add,
             )
 
+        def transpose(unit):
             pairs_t = t_banks.tile([P, 2, P], F32)
+            pairs_of[unit] = pairs_t
             for s in range(2):
                 nc.tensor.transpose(
                     out=pairs_t[:, s, :],
-                    in_=o_bf16[:, s].rearrange("p q e -> p (q e)").bitcast(F32),
+                    in_=o_bf16[:, unit, s].rearrange("p q e -> p (q e)").bitcast(F32),
                     identity=identity[:],
                 )
-            o_grouped = per_unit.tile([P, P * PACK], BF16, align_bytes=64)
-            nc.vector.tensor_copy(
-                out=o_grouped[:].bitcast(F32).rearrange("q (t s) -> q t s", s=2),
-                in_=pairs_t[:].rearrange("q s t -> q t s"),
-            )
-            o_codes = per_unit.tile([P, P], I32, align_bytes=64)
-            o_scales = per_unit.tile([P, P], U8, align_bytes=64)
-            nc.vector.quantize_mx(out=o_codes[:].bitcast(FP8X4), scales=o_scales[:], in_=o_grouped[:])
 
+        def regroup(unit):
+            nc.vector.tensor_copy(
+                out=o_grouped[:, unit, :].bitcast(F32).rearrange("q (t s) -> q t s", s=2),
+                in_=pairs_of[unit][:].rearrange("q s t -> q t s"),
+            )
+
+        def quantise(unit):
+            nc.vector.quantize_mx(
+                out=o_codes[:, unit, :].bitcast(FP8X4),
+                scales=o_scales[:, unit, :],
+                in_=o_grouped[:, unit, :],
+            )
+
+        def bilinear(unit):
+            h = unit // T_TILES
             q_bank = q_banks.tile([P, DH], F32)
+            q_bank_of[unit] = q_bank
             nc.tensor.matmul_mx(
                 out=q_bank[:],
-                lhsT=o_codes[:].bitcast(FP8X4),
-                lhsT_scale=o_scales[:],
+                lhsT=o_codes[:, unit, :].bitcast(FP8X4),
+                lhsT_scale=o_scales[:, unit, :],
                 rhs=atte_words[:, h, :].bitcast(FP8X4),
                 rhs_scale=atte_planes[4 * h : P, :],
                 start=True,
                 stop=True,
             )
-            q_f32 = per_unit.tile([P, DH], F32)
-            nc.scalar.copy(out=q_f32[:], in_=q_bank[:])
-            nc.sync.dma_start(out=out_1[0, h, steps, :], in_=q_f32[:])
+
+        def empty(unit):
+            h, steps = head_and_steps(unit)
+            nc.scalar.copy(out=q_f32[:, unit, :], in_=q_bank_of[unit][:])
+            nc.sync.dma_start(out=out_1[0, h, steps, :], in_=q_f32[:, unit, :])
+
+        stages = (
+            project, square, invert, root, normalise, round_to_bf16,
+            transpose, regroup, quantise, bilinear, empty,
+        )
+        for step in range(UNITS + len(stages) - 1):
+            for lag in reversed(range(len(stages))):
+                if 0 <= step - lag < UNITS:
+                    stages[lag](step - lag)

@@ -58,9 +58,8 @@ def tile_mca_pa_e_kernel(
             )
         proj_words = keep.tile([P, H * D_PASSES, DH], I32, align_bytes=64)
         proj_bytes = rgb_proj_words.rearrange("g p n t -> p g (n t)").bitcast(I32)
-        for h in range(H):
-            passes = slice(h * D_PASSES, (h + 1) * D_PASSES)
-            nc.sync.dma_start(out=proj_words[:, passes, :], in_=proj_bytes[:, passes, :])
+        for weight_pass in range(H * D_PASSES):
+            nc.sync.dma_start(out=proj_words[:, weight_pass, :], in_=proj_bytes[:, weight_pass, :])
         for quadrant in range(QUADRANTS):
             nc.sync.dma_start(
                 out=atte_planes[32 * quadrant : 32 * quadrant + 8, :].bitcast(I32),
@@ -178,7 +177,7 @@ def tile_mca_pa_e_kernel(
                 )
 
         def regroup(unit):
-            nc.vector.tensor_copy(
+            nc.scalar.copy(
                 out=o_grouped[:, unit, :].bitcast(F32).rearrange("q (t s) -> q t s", s=2),
                 in_=pairs_of[unit][:].rearrange("q s t -> q t s"),
             )

@@ -21,6 +21,7 @@ UNITS = H * T_TILES
 EPS = 1e-12
 QUADRANTS = 4
 HALF_T = T // 2
+WARM_PASSES = 12
 
 FLOPS = 2 * H * T * D * DH + 2 * H * T * DH * DH
 
@@ -46,6 +47,22 @@ def tile_mca_pa_e_kernel(
         nc.scalar.activation(out=warm[:], in_=one[:], func=ACT.Sqrt)
         identity = keep.tile([P, P], F32)
         make_identity(nc, identity[:])
+        zeros = keep.tile([P, DH * PACK], BF16, align_bytes=64)
+        zero_words = keep.tile([P, DH], I32, align_bytes=64)
+        zero_plane = keep.tile([P, DH], U8, align_bytes=64)
+        nc.vector.memset(zeros[:].bitcast(I32), 0)
+        nc.vector.quantize_mx(out=zero_words[:].bitcast(FP8X4), scales=zero_plane[:], in_=zeros[:])
+        warm_bank = q_banks.tile([P, DH], F32, tag="q_bank")
+        for warm_pass in range(WARM_PASSES):
+            nc.tensor.matmul_mx(
+                out=warm_bank[:],
+                lhsT=zero_words[:, :P].bitcast(FP8X4),
+                lhsT_scale=zero_plane[:, :P],
+                rhs=zero_words[:].bitcast(FP8X4),
+                rhs_scale=zero_plane[:],
+                start=True,
+                stop=True,
+            )
 
         rgb_raw = keep.tile([P, D_PASSES, PACK, T], BF16)
         rgb_rows = rgb.rearrange("o (g p j) w -> (o g) p j w", g=D_PASSES, p=P, j=PACK)

@@ -21,7 +21,7 @@ UNITS = H * T_TILES
 EPS = 1e-12
 QUADRANTS = 4
 HALF_T = T // 2
-WARM_PASSES = 12
+WARM_PASSES = 28
 
 FLOPS = 2 * H * T * D * DH + 2 * H * T * DH * DH
 
@@ -32,9 +32,8 @@ def tile_mca_pa_e_kernel(
     nc = tc.nc
     with ExitStack() as stack:
         keep = stack.enter_context(tc.tile_pool(name="keep", bufs=1))
-        p_banks = stack.enter_context(tc.psum_pool(name="p_banks", bufs=4))
+        sum_banks = stack.enter_context(tc.psum_pool(name="sum_banks", bufs=6))
         t_banks = stack.enter_context(tc.psum_pool(name="t_banks", bufs=2))
-        q_banks = stack.enter_context(tc.psum_pool(name="q_banks", bufs=2))
         stack.enter_context(tc.manual_schedule())
 
         proj_planes = keep.tile([P, DH], U8, align_bytes=64)
@@ -47,17 +46,17 @@ def tile_mca_pa_e_kernel(
         nc.scalar.activation(out=warm[:], in_=one[:], func=ACT.Sqrt)
         identity = keep.tile([P, P], F32)
         make_identity(nc, identity[:])
-        zeros = keep.tile([P, DH * PACK], BF16, align_bytes=64)
-        zero_words = keep.tile([P, DH], I32, align_bytes=64)
-        zero_plane = keep.tile([P, DH], U8, align_bytes=64)
+        zeros = keep.tile([P, P * PACK], BF16, align_bytes=64)
+        zero_words = keep.tile([P, P], I32, align_bytes=64)
+        zero_plane = keep.tile([P, P], U8, align_bytes=64)
         nc.vector.memset(zeros[:].bitcast(I32), 0)
         nc.vector.quantize_mx(out=zero_words[:].bitcast(FP8X4), scales=zero_plane[:], in_=zeros[:])
-        warm_bank = q_banks.tile([P, DH], F32, tag="q_bank")
+        warm_bank = sum_banks.tile([P, DH], F32, tag="sums")
         for warm_pass in range(WARM_PASSES):
             nc.tensor.matmul_mx(
-                out=warm_bank[:],
-                lhsT=zero_words[:, :P].bitcast(FP8X4),
-                lhsT_scale=zero_plane[:, :P],
+                out=warm_bank[:, :P],
+                lhsT=zero_words[:].bitcast(FP8X4),
+                lhsT_scale=zero_plane[:],
                 rhs=zero_words[:].bitcast(FP8X4),
                 rhs_scale=zero_plane[:],
                 start=True,
@@ -104,11 +103,14 @@ def tile_mca_pa_e_kernel(
                 in_=rgb_grouped[:, g, steps, :].rearrange("p w j -> p (w j)"),
             )
 
-        first_half, second_half = slice(0, HALF_T), slice(HALF_T, T)
+        early_tiles = [slice(t_tile * P, (t_tile + 1) * P) for t_tile in range(T_TILES // 2)]
+        second_half = slice(HALF_T, T)
         for g in range(D_PASSES):
-            regroup_rgb(nc.vector.tensor_copy, g, first_half)
+            for steps in early_tiles:
+                regroup_rgb(nc.vector.tensor_copy, g, steps)
             regroup_rgb(nc.scalar.copy, g, second_half)
-            quantise_rgb(g, first_half)
+            for steps in early_tiles:
+                quantise_rgb(g, steps)
         for g in range(D_PASSES):
             quantise_rgb(g, second_half)
 
@@ -131,7 +133,7 @@ def tile_mca_pa_e_kernel(
 
         def project(unit):
             h, steps = head_and_steps(unit)
-            p_bank = p_banks.tile([P, DH], F32)
+            p_bank = sum_banks.tile([P, DH], F32, tag="sums")
             p_bank_of[unit] = p_bank
             for g in range(D_PASSES):
                 weight_pass = h * D_PASSES + g
@@ -208,7 +210,7 @@ def tile_mca_pa_e_kernel(
 
         def bilinear(unit):
             h = unit // T_TILES
-            q_bank = q_banks.tile([P, DH], F32)
+            q_bank = sum_banks.tile([P, DH], F32, tag="sums")
             q_bank_of[unit] = q_bank
             nc.tensor.matmul_mx(
                 out=q_bank[:],

@@ -21,6 +21,7 @@ UNITS = H * T_TILES
 EPS = 1e-12
 QUADRANTS = 4
 HALF_T = T // 2
+VECTOR_REGROUPS = 3
 WARM_PASSES = 28
 
 FLOPS = 2 * H * T * D * DH + 2 * H * T * DH * DH
@@ -196,7 +197,8 @@ def tile_mca_pa_e_kernel(
                 )
 
         def regroup(unit):
-            nc.scalar.copy(
+            copy = nc.vector.tensor_copy if unit >= UNITS - VECTOR_REGROUPS else nc.scalar.copy
+            copy(
                 out=o_grouped[:, unit, :].bitcast(F32).rearrange("q (t s) -> q t s", s=2),
                 in_=pairs_of[unit][:].rearrange("q s t -> q t s"),
             )

@@ -22,6 +22,7 @@ EPS = 1e-12
 QUADRANTS = 4
 HALF_T = T // 2
 VECTOR_REGROUPS = 3
+VECTOR_ROUNDS = 2
 WARM_PASSES = 28
 
 FLOPS = 2 * H * T * D * DH + 2 * H * T * DH * DH
@@ -177,14 +178,18 @@ def tile_mca_pa_e_kernel(
             nc.sync.dma_start(out=out_0[0, h, steps, :], in_=o_f32[:, unit, :])
 
         def round_to_bf16(unit):
-            nc.gpsimd.tensor_scalar(
-                out=o_bf16[:, unit],
-                in0=o_f32[:, unit, :].rearrange("p (q s e) -> p s q e", s=2, e=2),
-                scalar1=1.0,
-                scalar2=0.0,
-                op0=ALU.mult,
-                op1=ALU.add,
-            )
+            pairs_first = o_f32[:, unit, :].rearrange("p (q s e) -> p s q e", s=2, e=2)
+            if unit >= UNITS - VECTOR_ROUNDS:
+                nc.vector.tensor_copy(out=o_bf16[:, unit], in_=pairs_first)
+            else:
+                nc.gpsimd.tensor_scalar(
+                    out=o_bf16[:, unit],
+                    in0=pairs_first,
+                    scalar1=1.0,
+                    scalar2=0.0,
+                    op0=ALU.mult,
+                    op1=ALU.add,
+                )
 
         def transpose(unit):
             pairs_t = t_banks.tile([P, 2, P], F32)

@@ -23,7 +23,7 @@ QUADRANTS = 4
 HALF_T = T // 2
 VECTOR_REGROUPS = 3
 VECTOR_ROUNDS = 2
-WARM_PASSES = 28
+WARM_PASSES = 40
 
 FLOPS = 2 * H * T * D * DH + 2 * H * T * DH * DH
 

@@ -23,6 +23,9 @@ QUADRANTS = 4
 HALF_T = T // 2
 VECTOR_REGROUPS = 3
 VECTOR_ROUNDS = 2
+SCALAR_NORMALISES = 1
+LAST_PIECES = 2
+EARLY_UNITS = 2
 WARM_PASSES = 40
 
 FLOPS = 2 * H * T * D * DH + 2 * H * T * DH * DH
@@ -133,14 +136,15 @@ def tile_mca_pa_e_kernel(
             h, t_tile = divmod(unit, T_TILES)
             return h, slice(t_tile * P, (t_tile + 1) * P)
 
-        def project(unit):
+        def project_passes(unit, passes):
             h, steps = head_and_steps(unit)
-            p_bank = sum_banks.tile([P, DH], F32, tag="sums")
-            p_bank_of[unit] = p_bank
-            for g in range(D_PASSES):
+            if unit not in p_bank_of:
+                p_bank = sum_banks.tile([P, DH], F32, tag="sums")
+                p_bank_of[unit] = p_bank
+            for g in passes:
                 weight_pass = h * D_PASSES + g
                 nc.tensor.matmul_mx(
-                    out=p_bank[:],
+                    out=p_bank_of[unit][:],
                     lhsT=rgb_codes[:, g, steps].bitcast(FP8X4),
                     lhsT_scale=rgb_scales[:, g, steps],
                     rhs=proj_words[:, weight_pass, :].bitcast(FP8X4),
@@ -148,6 +152,13 @@ def tile_mca_pa_e_kernel(
                     start=(g == 0),
                     stop=(g == D_PASSES - 1),
                 )
+
+        for unit in range(EARLY_UNITS):
+            project_passes(unit, range(D_PASSES - 1))
+
+        def project(unit):
+            first = D_PASSES - 1 if unit < EARLY_UNITS else 0
+            project_passes(unit, range(first, D_PASSES))
 
         def square(unit):
             nc.scalar.activation(
@@ -170,11 +181,19 @@ def tile_mca_pa_e_kernel(
 
         def normalise(unit):
             h, steps = head_and_steps(unit)
-            nc.vector.tensor_scalar_mul(
-                out=o_f32[:, unit, :],
-                in0=p_bank_of[unit][:],
-                scalar1=inverse_norm[:, unit : unit + 1],
-            )
+            if unit >= UNITS - SCALAR_NORMALISES:
+                nc.scalar.activation(
+                    out=o_f32[:, unit, :],
+                    in_=p_bank_of[unit][:],
+                    func=ACT.Copy,
+                    scale=inverse_norm[:, unit : unit + 1],
+                )
+            else:
+                nc.vector.tensor_scalar_mul(
+                    out=o_f32[:, unit, :],
+                    in0=p_bank_of[unit][:],
+                    scalar1=inverse_norm[:, unit : unit + 1],
+                )
             nc.sync.dma_start(out=out_0[0, h, steps, :], in_=o_f32[:, unit, :])
 
         def round_to_bf16(unit):
@@ -215,24 +234,36 @@ def tile_mca_pa_e_kernel(
                 in_=o_grouped[:, unit, :],
             )
 
+        def column_pieces(unit):
+            pieces = LAST_PIECES if unit == UNITS - 1 else 1
+            width = DH // pieces
+            return [slice(piece * width, (piece + 1) * width) for piece in range(pieces)]
+
         def bilinear(unit):
             h = unit // T_TILES
-            q_bank = sum_banks.tile([P, DH], F32, tag="sums")
-            q_bank_of[unit] = q_bank
-            nc.tensor.matmul_mx(
-                out=q_bank[:],
-                lhsT=o_codes[:, unit, :].bitcast(FP8X4),
-                lhsT_scale=o_scales[:, unit, :],
-                rhs=atte_words[:, h, :].bitcast(FP8X4),
-                rhs_scale=atte_planes[4 * h : P, :],
-                start=True,
-                stop=True,
-            )
+            q_bank_of[unit] = []
+            for columns in column_pieces(unit):
+                q_bank = sum_banks.tile([P, DH], F32, tag="sums")
+                q_bank_of[unit].append(q_bank)
+                nc.tensor.matmul_mx(
+                    out=q_bank[:, : columns.stop - columns.start],
+                    lhsT=o_codes[:, unit, :].bitcast(FP8X4),
+                    lhsT_scale=o_scales[:, unit, :],
+                    rhs=atte_words[:, h, columns].bitcast(FP8X4),
+                    rhs_scale=atte_planes[4 * h : P, columns],
+                    start=True,
+                    stop=True,
+                )
 
         def empty(unit):
             h, steps = head_and_steps(unit)
-            nc.scalar.copy(out=q_f32[:, unit, :], in_=q_bank_of[unit][:])
-            nc.sync.dma_start(out=out_1[0, h, steps, :], in_=q_f32[:, unit, :])
+            copies = (nc.scalar.copy, nc.vector.tensor_copy)
+            for piece, columns in enumerate(column_pieces(unit)):
+                copies[piece](
+                    out=q_f32[:, unit, columns],
+                    in_=q_bank_of[unit][piece][:, : columns.stop - columns.start],
+                )
+                nc.sync.dma_start(out=out_1[0, h, steps, columns], in_=q_f32[:, unit, columns])
 
         stages = (
             project, square, invert, root, normalise, round_to_bf16,

from contextlib import ExitStack

import concourse.mybir as mybir
from concourse.masks import make_identity

F32 = mybir.dt.float32
BF16 = mybir.dt.bfloat16
I32 = mybir.dt.int32
U8 = mybir.dt.uint8
FP8X4 = mybir.dt.float8_e4m3fn_x4
ACT = mybir.ActivationFunctionType
ALU = mybir.AluOpType

P = 128
PACK = 4
K_PASS = P * PACK
D, T, H, DH = 1024, 512, 2, 512
D_PASSES = D // K_PASS
T_TILES = T // P
UNITS = H * T_TILES
EPS = 1e-12
QUADRANTS = 4
HALF_T = T // 2
VECTOR_REGROUPS = 3
VECTOR_ROUNDS = 2
SCALAR_NORMALISES = 1
LAST_PIECES = 2
EARLY_UNITS = 2
WARM_PASSES = 40

FLOPS = 2 * H * T * D * DH + 2 * H * T * DH * DH


def tile_mca_pa_e_kernel(
    tc, rgb, rgb_proj_words, rgb_proj_scales, atte_w_words, atte_w_scales, out_0, out_1
):
    nc = tc.nc
    with ExitStack() as stack:
        keep = stack.enter_context(tc.tile_pool(name="keep", bufs=1))
        sum_banks = stack.enter_context(tc.psum_pool(name="sum_banks", bufs=6))
        t_banks = stack.enter_context(tc.psum_pool(name="t_banks", bufs=2))
        stack.enter_context(tc.manual_schedule())

        proj_planes = keep.tile([P, DH], U8, align_bytes=64)
        atte_planes = keep.tile([P, DH], U8, align_bytes=64)
        nc.vector.memset(proj_planes[:].bitcast(I32), 0)
        nc.vector.memset(atte_planes[:].bitcast(I32), 0)
        one = keep.tile([P, 1], F32)
        warm = keep.tile([P, 1], F32)
        nc.vector.memset(one[:], 1.0)
        nc.scalar.activation(out=warm[:], in_=one[:], func=ACT.Sqrt)
        identity = keep.tile([P, P], F32)
        make_identity(nc, identity[:])
        zeros = keep.tile([P, P * PACK], BF16, align_bytes=64)
        zero_words = keep.tile([P, P], I32, align_bytes=64)
        zero_plane = keep.tile([P, P], U8, align_bytes=64)
        nc.vector.memset(zeros[:].bitcast(I32), 0)
        nc.vector.quantize_mx(out=zero_words[:].bitcast(FP8X4), scales=zero_plane[:], in_=zeros[:])
        warm_bank = sum_banks.tile([P, DH], F32, tag="sums")
        for warm_pass in range(WARM_PASSES):
            nc.tensor.matmul_mx(
                out=warm_bank[:, :P],
                lhsT=zero_words[:].bitcast(FP8X4),
                lhsT_scale=zero_plane[:],
                rhs=zero_words[:].bitcast(FP8X4),
                rhs_scale=zero_plane[:],
                start=True,
                stop=True,
            )

        rgb_raw = keep.tile([P, D_PASSES, PACK, T], BF16)
        rgb_rows = rgb.rearrange("o (g p j) w -> (o g) p j w", g=D_PASSES, p=P, j=PACK)
        for g in range(D_PASSES):
            nc.sync.dma_start(out=rgb_raw[:, g], in_=rgb_rows[g])
        for quadrant in range(QUADRANTS):
            nc.sync.dma_start(
                out=proj_planes[32 * quadrant : 32 * quadrant + 16, :].bitcast(I32),
                in_=rgb_proj_scales[:, 4 * quadrant : 4 * quadrant + 4, :].bitcast(I32),
            )
        proj_words = keep.tile([P, H * D_PASSES, DH], I32, align_bytes=64)
        proj_bytes = rgb_proj_words.rearrange("g p n t -> p g (n t)").bitcast(I32)
        for weight_pass in range(H * D_PASSES):
            nc.sync.dma_start(out=proj_words[:, weight_pass, :], in_=proj_bytes[:, weight_pass, :])
        for quadrant in range(QUADRANTS):
            nc.sync.dma_start(
                out=atte_planes[32 * quadrant : 32 * quadrant + 8, :].bitcast(I32),
                in_=atte_w_scales[:, 4 * quadrant : 4 * quadrant + 4, :].bitcast(I32),
            )
        atte_words = keep.tile([P, H, DH], I32, align_bytes=64)
        nc.sync.dma_start(
            out=atte_words[:], in_=atte_w_words.rearrange("g p n t -> p g (n t)").bitcast(I32)
        )

        rgb_grouped = keep.tile([P, D_PASSES, T, PACK], BF16, align_bytes=64)
        rgb_codes = keep.tile([P, D_PASSES, T], I32, align_bytes=64)
        rgb_scales = keep.tile([P, D_PASSES, T], U8, align_bytes=64)

        def regroup_rgb(copy, g, steps):
            copy(
                out=rgb_grouped[:, g, steps, :],
                in_=rgb_raw[:, g, :, steps].rearrange("p j w -> p w j"),
            )

        def quantise_rgb(g, steps):
            nc.vector.quantize_mx(
                out=rgb_codes[:, g, steps].bitcast(FP8X4),
                scales=rgb_scales[:, g, steps],
                in_=rgb_grouped[:, g, steps, :].rearrange("p w j -> p (w j)"),
            )

        early_tiles = [slice(t_tile * P, (t_tile + 1) * P) for t_tile in range(T_TILES // 2)]
        second_half = slice(HALF_T, T)
        for g in range(D_PASSES):
            for steps in early_tiles:
                regroup_rgb(nc.vector.tensor_copy, g, steps)
            regroup_rgb(nc.scalar.copy, g, second_half)
            for steps in early_tiles:
                quantise_rgb(g, steps)
        for g in range(D_PASSES):
            quantise_rgb(g, second_half)

        squares = keep.tile([P, UNITS, DH], BF16)
        sum_squares = keep.tile([P, UNITS], F32)
        floored = keep.tile([P, UNITS], F32)
        inverse = keep.tile([P, UNITS], F32)
        inverse_norm = keep.tile([P, UNITS], F32)
        o_f32 = keep.tile([P, UNITS, DH], F32)
        o_bf16 = keep.tile([P, UNITS, 2, P, 2], BF16)
        o_grouped = keep.tile([P, UNITS, P * PACK], BF16, align_bytes=64)
        o_codes = keep.tile([P, UNITS, P], I32, align_bytes=64)
        o_scales = keep.tile([P, UNITS, P], U8, align_bytes=64)
        q_f32 = keep.tile([P, UNITS, DH], F32)
        p_bank_of, pairs_of, q_bank_of = {}, {}, {}

        def head_and_steps(unit):
            h, t_tile = divmod(unit, T_TILES)
            return h, slice(t_tile * P, (t_tile + 1) * P)

        def project_passes(unit, passes):
            h, steps = head_and_steps(unit)
            if unit not in p_bank_of:
                p_bank = sum_banks.tile([P, DH], F32, tag="sums")
                p_bank_of[unit] = p_bank
            for g in passes:
                weight_pass = h * D_PASSES + g
                nc.tensor.matmul_mx(
                    out=p_bank_of[unit][:],
                    lhsT=rgb_codes[:, g, steps].bitcast(FP8X4),
                    lhsT_scale=rgb_scales[:, g, steps],
                    rhs=proj_words[:, weight_pass, :].bitcast(FP8X4),
                    rhs_scale=proj_planes[4 * weight_pass : P, :],
                    start=(g == 0),
                    stop=(g == D_PASSES - 1),
                )

        for unit in range(EARLY_UNITS):
            project_passes(unit, range(D_PASSES - 1))

        def project(unit):
            first = D_PASSES - 1 if unit < EARLY_UNITS else 0
            project_passes(unit, range(first, D_PASSES))

        def square(unit):
            nc.scalar.activation(
                out=squares[:, unit, :],
                in_=p_bank_of[unit][:],
                func=ACT.Square,
                accum_out=sum_squares[:, unit : unit + 1],
            )

        def invert(unit):
            column = slice(unit, unit + 1)
            nc.vector.tensor_scalar_max(
                out=floored[:, column], in0=sum_squares[:, column], scalar1=EPS * EPS
            )
            nc.vector.reciprocal(out=inverse[:, column], in_=floored[:, column])

        def root(unit):
            column = slice(unit, unit + 1)
            nc.scalar.activation(out=inverse_norm[:, column], in_=inverse[:, column], func=ACT.Sqrt)

        def normalise(unit):
            h, steps = head_and_steps(unit)
            if unit >= UNITS - SCALAR_NORMALISES:
                nc.scalar.activation(
                    out=o_f32[:, unit, :],
                    in_=p_bank_of[unit][:],
                    func=ACT.Copy,
                    scale=inverse_norm[:, unit : unit + 1],
                )
            else:
                nc.vector.tensor_scalar_mul(
                    out=o_f32[:, unit, :],
                    in0=p_bank_of[unit][:],
                    scalar1=inverse_norm[:, unit : unit + 1],
                )
            nc.sync.dma_start(out=out_0[0, h, steps, :], in_=o_f32[:, unit, :])

        def round_to_bf16(unit):
            pairs_first = o_f32[:, unit, :].rearrange("p (q s e) -> p s q e", s=2, e=2)
            if unit >= UNITS - VECTOR_ROUNDS:
                nc.vector.tensor_copy(out=o_bf16[:, unit], in_=pairs_first)
            else:
                nc.gpsimd.tensor_scalar(
                    out=o_bf16[:, unit],
                    in0=pairs_first,
                    scalar1=1.0,
                    scalar2=0.0,
                    op0=ALU.mult,
                    op1=ALU.add,
                )

        def transpose(unit):
            pairs_t = t_banks.tile([P, 2, P], F32)
            pairs_of[unit] = pairs_t
            for s in range(2):
                nc.tensor.transpose(
                    out=pairs_t[:, s, :],
                    in_=o_bf16[:, unit, s].rearrange("p q e -> p (q e)").bitcast(F32),
                    identity=identity[:],
                )

        def regroup(unit):
            copy = nc.vector.tensor_copy if unit >= UNITS - VECTOR_REGROUPS else nc.scalar.copy
            copy(
                out=o_grouped[:, unit, :].bitcast(F32).rearrange("q (t s) -> q t s", s=2),
                in_=pairs_of[unit][:].rearrange("q s t -> q t s"),
            )

        def quantise(unit):
            nc.vector.quantize_mx(
                out=o_codes[:, unit, :].bitcast(FP8X4),
                scales=o_scales[:, unit, :],
                in_=o_grouped[:, unit, :],
            )

        def column_pieces(unit):
            pieces = LAST_PIECES if unit == UNITS - 1 else 1
            width = DH // pieces
            return [slice(piece * width, (piece + 1) * width) for piece in range(pieces)]

        def bilinear(unit):
            h = unit // T_TILES
            q_bank_of[unit] = []
            for columns in column_pieces(unit):
                q_bank = sum_banks.tile([P, DH], F32, tag="sums")
                q_bank_of[unit].append(q_bank)
                nc.tensor.matmul_mx(
                    out=q_bank[:, : columns.stop - columns.start],
                    lhsT=o_codes[:, unit, :].bitcast(FP8X4),
                    lhsT_scale=o_scales[:, unit, :],
                    rhs=atte_words[:, h, columns].bitcast(FP8X4),
                    rhs_scale=atte_planes[4 * h : P, columns],
                    start=True,
                    stop=True,
                )

        def empty(unit):
            h, steps = head_and_steps(unit)
            copies = (nc.scalar.copy, nc.vector.tensor_copy)
            for piece, columns in enumerate(column_pieces(unit)):
                copies[piece](
                    out=q_f32[:, unit, columns],
                    in_=q_bank_of[unit][piece][:, : columns.stop - columns.start],
                )
                nc.sync.dma_start(out=out_1[0, h, steps, columns], in_=q_f32[:, unit, columns])

        stages = (
            project, square, invert, root, normalise, round_to_bf16,
            transpose, regroup, quantise, bilinear, empty,
        )
        for step in range(UNITS + len(stages) - 1):
            for lag in reversed(range(len(stages))):
                if 0 <= step - lag < UNITS:
                    stages[lag](step - lag)
